import numpy as np
import ml_dtypes

BF16 = ml_dtypes.bfloat16


def bf(x):
    return np.asarray(x, np.float32).astype(BF16)


def f32(x):
    return np.asarray(x, np.float32)


def f64(x):
    return np.asarray(x).astype(np.float64)


def striped(idx):
    return np.tile(idx.reshape(-1, 16).T, (8, 1))


D, S, M, L, T, N = 128, 1024, 256, 512, 4, 2048


def setup_inputs():
    return {"table": bf(0.1 * np.random.standard_normal((D, S))), "kb": bf(np.random.standard_normal((D, M))), "offs": striped(np.random.permutation(np.tile(np.arange(S), 2))[:N])}


def reference(table, kb, offs):
    idx = offs[:16].T.reshape(-1)
    u = f64(kb).T @ f64(table)[:, idx]
    att = u.reshape(M, T, L).sum(axis=1)
    e = np.exp(att - att.max(axis=0, keepdims=True))
    p = e / e.sum(axis=0, keepdims=True)
    return f64(kb) @ p

@@ -1,0 +1,116 @@
+import concourse.mybir as mybir
+from concourse.masks import make_identity
+
+BF16, F32, U16 = mybir.dt.bfloat16, mybir.dt.float32, mybir.dt.uint16
+EXP = mybir.ActivationFunctionType.Exp
+MULT = mybir.AluOpType.mult
+X = mybir.AxisListType.X
+
+P = 128
+WORDS = 1024
+ENTRIES = 256
+SPANS = 512
+BAG = 4
+LIST = BAG * SPANS
+ENTRY_BLOCKS = ENTRIES // P
+SPAN_BLOCKS = SPANS // P
+PIECE = SPANS // 16
+
+FLOPS = 2 * P * ENTRIES * LIST + 2 * P * ENTRIES * SPANS
+
+
+def tile_encodertreespannn_kernel(tc, table, kb, offs, out):
+    nc = tc.nc
+    with (
+        tc.tile_pool(name="held", bufs=1) as held,
+        tc.psum_pool(name="banks", bufs=1) as banks,
+    ):
+        offsets = held.tile([P, LIST // 16], U16, name="offsets")
+        nc.sync.dma_start(offsets[:], offs)
+        kb_sb = held.tile([P, ENTRIES], BF16, name="kb_sb")
+        nc.scalar.dma_start(kb_sb[:], kb)
+        table_sb = held.tile([P, WORDS], BF16, name="table_sb")
+        nc.sync.dma_start(table_sb[:], table)
+
+        ident_f32 = held.tile([P, P], F32, name="ident_f32")
+        make_identity(nc, ident_f32[:])
+        ident_bf16 = held.tile([P, P], BF16, name="ident_bf16")
+        make_identity(nc, ident_bf16[:])
+        warm = held.tile([P, 1], F32, name="warm")
+        nc.vector.memset(warm[:], 0.0)
+        warm_out = held.tile([P, 1], F32, name="warm_out")
+        nc.scalar.activation(warm_out[:], warm[:], EXP)
+
+        kbT_ps = banks.tile([P, ENTRIES], BF16, name="kbT_ps")
+        for mb in range(ENTRY_BLOCKS):
+            nc.tensor.transpose(
+                kbT_ps[:, mb * P : (mb + 1) * P], kb_sb[:, mb * P : (mb + 1) * P], ident_bf16[:]
+            )
+        kbT_sb = held.tile([P, ENTRIES], BF16, name="kbT_sb")
+        nc.vector.tensor_copy(kbT_sb[:], kbT_ps[:])
+
+        att_sb = []
+        for mb in range(ENTRY_BLOCKS):
+            att_ps = banks.tile([P, SPANS], F32, name=f"att_ps{mb}", tag=f"wide{mb}")
+            for t in range(BAG):
+                nc.tensor.matmul(
+                    att_ps[:],
+                    kb_sb[:, mb * P : (mb + 1) * P],
+                    table_sb[:].indirect(offsets[:, t * PIECE : (t + 1) * PIECE]),
+                    start=(t == 0),
+                    stop=(t == BAG - 1),
+                )
+            att_sb.append(held.tile([P, SPANS], F32, name=f"att_sb{mb}"))
+            if mb == 0:
+                nc.scalar.copy(att_sb[mb][:], att_ps[:])
+            else:
+                nc.vector.tensor_copy(att_sb[mb][:], att_ps[:])
+
+        attT_ps = [banks.tile([P, ENTRIES], F32, name=f"attT_ps{b}") for b in range(SPAN_BLOCKS)]
+        for mb in range(ENTRY_BLOCKS):
+            for b in range(SPAN_BLOCKS):
+                nc.tensor.transpose(
+                    attT_ps[b][:, mb * P : (mb + 1) * P],
+                    att_sb[mb][:, b * P : (b + 1) * P],
+                    ident_f32[:],
+                )
+
+        neg_max = held.tile([P, SPAN_BLOCKS], F32, name="neg_max")
+        total = held.tile([P, SPAN_BLOCKS], F32, name="total")
+        inverse = held.tile([P, SPAN_BLOCKS], F32, name="inverse")
+        p_ps = [
+            banks.tile([P, SPANS], BF16, name=f"p_ps{mb}", tag=f"wide{mb}")
+            for mb in range(ENTRY_BLOCKS)
+        ]
+        for b in range(SPAN_BLOCKS):
+            one = slice(b, b + 1)
+            nc.vector.reduce_max(neg_max[:, one], attT_ps[b][:], X, negate=True)
+            e_sb = held.tile([P, ENTRIES], F32, name=f"e_sb{b}")
+            nc.scalar.activation(
+                e_sb[:], attT_ps[b][:], EXP, bias=neg_max[:, one], accum_out=total[:, one]
+            )
+            nc.vector.reciprocal(inverse[:, one], total[:, one])
+            pT_sb = held.tile([P, ENTRIES], BF16, name=f"pT_sb{b}")
+            nc.vector.tensor_scalar(pT_sb[:], e_sb[:], inverse[:, one], None, MULT)
+            for mb in range(ENTRY_BLOCKS):
+                nc.tensor.transpose(
+                    p_ps[mb][:, b * P : (b + 1) * P], pT_sb[:, mb * P : (mb + 1) * P], ident_bf16[:]
+                )
+
+        out_ps = banks.tile([P, SPANS], F32, name="out_ps")
+        for mb in range(ENTRY_BLOCKS):
+            p_sb = held.tile([P, SPANS], BF16, name=f"p_sb{mb}")
+            if mb == 0:
+                nc.scalar.copy(p_sb[:], p_ps[mb][:])
+            else:
+                nc.vector.tensor_copy(p_sb[:], p_ps[mb][:])
+            nc.tensor.matmul(
+                out_ps[:],
+                kbT_sb[:, mb * P : (mb + 1) * P],
+                p_sb[:],
+                start=(mb == 0),
+                stop=(mb == ENTRY_BLOCKS - 1),
+            )
+        out_sb = held.tile([P, SPANS], F32, name="out_sb")
+        nc.vector.tensor_copy(out_sb[:], out_ps[:])
+        nc.sync.dma_start(out, out_sb[:])

@@ -14,7 +14,9 @@ BAG = 4
 LIST = BAG * SPANS
 ENTRY_BLOCKS = ENTRIES // P
 SPAN_BLOCKS = SPANS // P
-PIECE = SPANS // 16
+HALVES = 2
+HALF = SPANS // HALVES
+HALF_BLOCKS = HALF // P
 
 FLOPS = 2 * P * ENTRIES * LIST + 2 * P * ENTRIES * SPANS
 
@@ -41,7 +43,8 @@ def tile_encodertreespannn_kernel(tc, table, kb, offs, out):
         warm_out = held.tile([P, 1], F32, name="warm_out")
         nc.scalar.activation(warm_out[:], warm[:], EXP)
 
-        kbT_ps = banks.tile([P, ENTRIES], BF16, name="kbT_ps")
+
+        kbT_ps = banks.tile([P, ENTRIES], BF16, name="kbT_ps", tag="flip3")
         for mb in range(ENTRY_BLOCKS):
             nc.tensor.transpose(
                 kbT_ps[:, mb * P : (mb + 1) * P], kb_sb[:, mb * P : (mb + 1) * P], ident_bf16[:]
@@ -49,40 +52,41 @@ def tile_encodertreespannn_kernel(tc, table, kb, offs, out):
         kbT_sb = held.tile([P, ENTRIES], BF16, name="kbT_sb")
         nc.vector.tensor_copy(kbT_sb[:], kbT_ps[:])
 
-        att_sb = []
-        for mb in range(ENTRY_BLOCKS):
-            att_ps = banks.tile([P, SPANS], F32, name=f"att_ps{mb}", tag=f"wide{mb}")
-            for t in range(BAG):
-                nc.tensor.matmul(
-                    att_ps[:],
-                    kb_sb[:, mb * P : (mb + 1) * P],
-                    table_sb[:].indirect(offsets[:, t * PIECE : (t + 1) * PIECE]),
-                    start=(t == 0),
-                    stop=(t == BAG - 1),
-                )
-            att_sb.append(held.tile([P, SPANS], F32, name=f"att_sb{mb}"))
-            if mb == 0:
-                nc.scalar.copy(att_sb[mb][:], att_ps[:])
-            else:
-                nc.vector.tensor_copy(att_sb[mb][:], att_ps[:])
-
-        attT_ps = [banks.tile([P, ENTRIES], F32, name=f"attT_ps{b}") for b in range(SPAN_BLOCKS)]
-        for mb in range(ENTRY_BLOCKS):
-            for b in range(SPAN_BLOCKS):
-                nc.tensor.transpose(
-                    attT_ps[b][:, mb * P : (mb + 1) * P],
-                    att_sb[mb][:, b * P : (b + 1) * P],
-                    ident_f32[:],
-                )
-
+        att_sb = {}
+        attT_ps = {}
         neg_max = held.tile([P, SPAN_BLOCKS], F32, name="neg_max")
         total = held.tile([P, SPAN_BLOCKS], F32, name="total")
         inverse = held.tile([P, SPAN_BLOCKS], F32, name="inverse")
-        p_ps = [
-            banks.tile([P, SPANS], BF16, name=f"p_ps{mb}", tag=f"wide{mb}")
-            for mb in range(ENTRY_BLOCKS)
-        ]
-        for b in range(SPAN_BLOCKS):
+
+        def scores(h, mb):
+            att_ps = banks.tile([P, HALF], F32, name=f"att_ps{h}{mb}", tag=f"att{h}{mb}")
+            for t in range(BAG):
+                first = (t * SPANS + h * HALF) // 16
+                nc.tensor.matmul(
+                    att_ps[:],
+                    kb_sb[:, mb * P : (mb + 1) * P],
+                    table_sb[:].indirect(offsets[:, first : first + HALF // 16]),
+                    start=(t == 0),
+                    stop=(t == BAG - 1),
+                )
+            att_sb[h, mb] = held.tile([P, HALF], F32, name=f"att_sb{h}{mb}")
+            if mb == 0:
+                nc.scalar.copy(att_sb[h, mb][:], att_ps[:])
+            else:
+                nc.vector.tensor_copy(att_sb[h, mb][:], att_ps[:])
+
+        def flip(h):
+            for i in range(HALF_BLOCKS):
+                b = h * HALF_BLOCKS + i
+                attT_ps[b] = banks.tile([P, ENTRIES], F32, name=f"attT_ps{b}", tag=f"flip{b}")
+                for mb in range(ENTRY_BLOCKS):
+                    nc.tensor.transpose(
+                        attT_ps[b][:, mb * P : (mb + 1) * P],
+                        att_sb[h, mb][:, i * P : (i + 1) * P],
+                        ident_f32[:],
+                    )
+
+        def read_out(b):
             one = slice(b, b + 1)
             nc.vector.reduce_max(neg_max[:, one], attT_ps[b][:], X, negate=True)
             e_sb = held.tile([P, ENTRIES], F32, name=f"e_sb{b}")
@@ -92,25 +96,33 @@ def tile_encodertreespannn_kernel(tc, table, kb, offs, out):
             nc.vector.reciprocal(inverse[:, one], total[:, one])
             pT_sb = held.tile([P, ENTRIES], BF16, name=f"pT_sb{b}")
             nc.vector.tensor_scalar(pT_sb[:], e_sb[:], inverse[:, one], None, MULT)
+            p_ps = banks.tile(
+                [P, ENTRIES], BF16, name=f"p_ps{b}", tag=f"att{b // HALF_BLOCKS}{b % HALF_BLOCKS}"
+            )
             for mb in range(ENTRY_BLOCKS):
                 nc.tensor.transpose(
-                    p_ps[mb][:, b * P : (b + 1) * P], pT_sb[:, mb * P : (mb + 1) * P], ident_bf16[:]
+                    p_ps[:, mb * P : (mb + 1) * P], pT_sb[:, mb * P : (mb + 1) * P], ident_bf16[:]
                 )
+            p_sb = held.tile([P, ENTRIES], BF16, name=f"p_sb{b}")
+            nc.scalar.copy(p_sb[:], p_ps[:])
+            out_ps = banks.tile([P, P], F32, name=f"out_ps{b}", tag=f"flip{b}")
+            for mb in range(ENTRY_BLOCKS):
+                nc.tensor.matmul(
+                    out_ps[:],
+                    kbT_sb[:, mb * P : (mb + 1) * P],
+                    p_sb[:, mb * P : (mb + 1) * P],
+                    start=(mb == 0),
+                    stop=(mb == ENTRY_BLOCKS - 1),
+                )
+            out_sb = held.tile([P, P], F32, name=f"out_sb{b}")
+            nc.vector.tensor_copy(out_sb[:], out_ps[:])
+            nc.sync.dma_start(out[:, b * P : (b + 1) * P], out_sb[:])
 
-        out_ps = banks.tile([P, SPANS], F32, name="out_ps")
-        for mb in range(ENTRY_BLOCKS):
-            p_sb = held.tile([P, SPANS], BF16, name=f"p_sb{mb}")
-            if mb == 0:
-                nc.scalar.copy(p_sb[:], p_ps[mb][:])
-            else:
-                nc.vector.tensor_copy(p_sb[:], p_ps[mb][:])
-            nc.tensor.matmul(
-                out_ps[:],
-                kbT_sb[:, mb * P : (mb + 1) * P],
-                p_sb[:],
-                start=(mb == 0),
-                stop=(mb == ENTRY_BLOCKS - 1),
-            )
-        out_sb = held.tile([P, SPANS], F32, name="out_sb")
-        nc.vector.tensor_copy(out_sb[:], out_ps[:])
-        nc.sync.dma_start(out, out_sb[:])
+        scores(0, 0)
+        scores(0, 1)
+        scores(1, 0)
+        flip(0)
+        scores(1, 1)
+        flip(1)
+        for b in range(SPAN_BLOCKS):
+            read_out(b)

@@ -17,6 +17,7 @@ SPAN_BLOCKS = SPANS // P
 HALVES = 2
 HALF = SPANS // HALVES
 HALF_BLOCKS = HALF // P
+WARM_UP = 3
 
 FLOPS = 2 * P * ENTRIES * LIST + 2 * P * ENTRIES * SPANS
 
@@ -34,6 +35,8 @@ def tile_encodertreespannn_kernel(tc, table, kb, offs, out):
         table_sb = held.tile([P, WORDS], BF16, name="table_sb")
         nc.sync.dma_start(table_sb[:], table)
 
+        zeros = held.tile([P, SPANS], BF16, name="zeros")
+        nc.vector.memset(zeros[:], 0.0)
         ident_f32 = held.tile([P, P], F32, name="ident_f32")
         make_identity(nc, ident_f32[:])
         ident_bf16 = held.tile([P, P], BF16, name="ident_bf16")
@@ -42,6 +45,10 @@ def tile_encodertreespannn_kernel(tc, table, kb, offs, out):
         nc.vector.memset(warm[:], 0.0)
         warm_out = held.tile([P, 1], F32, name="warm_out")
         nc.scalar.activation(warm_out[:], warm[:], EXP)
+
+        idle_ps = banks.tile([P, SPANS], F32, name="idle_ps", tag="att11")
+        for i in range(WARM_UP):
+            nc.tensor.matmul(idle_ps[:], zeros[:, 0:P], zeros[:], start=True, stop=True)
 
 
         kbT_ps = banks.tile([P, ENTRIES], BF16, name="kbT_ps", tag="flip3")

@@ -17,7 +17,7 @@ SPAN_BLOCKS = SPANS // P
 HALVES = 2
 HALF = SPANS // HALVES
 HALF_BLOCKS = HALF // P
-WARM_UP = 3
+LOADS = 4
 
 FLOPS = 2 * P * ENTRIES * LIST + 2 * P * ENTRIES * SPANS
 
@@ -33,10 +33,11 @@ def tile_encodertreespannn_kernel(tc, table, kb, offs, out):
         kb_sb = held.tile([P, ENTRIES], BF16, name="kb_sb")
         nc.scalar.dma_start(kb_sb[:], kb)
         table_sb = held.tile([P, WORDS], BF16, name="table_sb")
-        nc.sync.dma_start(table_sb[:], table)
+        for q in range(LOADS):
+            columns = slice(q * (WORDS // LOADS), (q + 1) * (WORDS // LOADS))
+            queue = nc.sync if q % 2 == 0 else nc.scalar
+            queue.dma_start(table_sb[:, columns], table[:, columns])
 
-        zeros = held.tile([P, SPANS], BF16, name="zeros")
-        nc.vector.memset(zeros[:], 0.0)
         ident_f32 = held.tile([P, P], F32, name="ident_f32")
         make_identity(nc, ident_f32[:])
         ident_bf16 = held.tile([P, P], BF16, name="ident_bf16")
@@ -45,10 +46,6 @@ def tile_encodertreespannn_kernel(tc, table, kb, offs, out):
         nc.vector.memset(warm[:], 0.0)
         warm_out = held.tile([P, 1], F32, name="warm_out")
         nc.scalar.activation(warm_out[:], warm[:], EXP)
-
-        idle_ps = banks.tile([P, SPANS], F32, name="idle_ps", tag="att11")
-        for i in range(WARM_UP):
-            nc.tensor.matmul(idle_ps[:], zeros[:, 0:P], zeros[:], start=True, stop=True)
 
 
         kbT_ps = banks.tile([P, ENTRIES], BF16, name="kbT_ps", tag="flip3")

@@ -17,7 +17,6 @@ SPAN_BLOCKS = SPANS // P
 HALVES = 2
 HALF = SPANS // HALVES
 HALF_BLOCKS = HALF // P
-LOADS = 4
 
 FLOPS = 2 * P * ENTRIES * LIST + 2 * P * ENTRIES * SPANS
 
@@ -33,10 +32,7 @@ def tile_encodertreespannn_kernel(tc, table, kb, offs, out):
         kb_sb = held.tile([P, ENTRIES], BF16, name="kb_sb")
         nc.scalar.dma_start(kb_sb[:], kb)
         table_sb = held.tile([P, WORDS], BF16, name="table_sb")
-        for q in range(LOADS):
-            columns = slice(q * (WORDS // LOADS), (q + 1) * (WORDS // LOADS))
-            queue = nc.sync if q % 2 == 0 else nc.scalar
-            queue.dma_start(table_sb[:, columns], table[:, columns])
+        nc.sync.dma_start(table_sb[:], table)
 
         ident_f32 = held.tile([P, P], F32, name="ident_f32")
         make_identity(nc, ident_f32[:])
@@ -92,34 +88,35 @@ def tile_encodertreespannn_kernel(tc, table, kb, offs, out):
 
         def read_out(b):
             one = slice(b, b + 1)
+            att_bank = f"att{b // HALF_BLOCKS}{b % HALF_BLOCKS}"
             nc.vector.reduce_max(neg_max[:, one], attT_ps[b][:], X, negate=True)
-            e_sb = held.tile([P, ENTRIES], F32, name=f"e_sb{b}")
+            eT_sb = held.tile([P, ENTRIES], BF16, name=f"eT_sb{b}")
             nc.scalar.activation(
-                e_sb[:], attT_ps[b][:], EXP, bias=neg_max[:, one], accum_out=total[:, one]
+                eT_sb[:], attT_ps[b][:], EXP, bias=neg_max[:, one], accum_out=total[:, one]
             )
-            nc.vector.reciprocal(inverse[:, one], total[:, one])
-            pT_sb = held.tile([P, ENTRIES], BF16, name=f"pT_sb{b}")
-            nc.vector.tensor_scalar(pT_sb[:], e_sb[:], inverse[:, one], None, MULT)
-            p_ps = banks.tile(
-                [P, ENTRIES], BF16, name=f"p_ps{b}", tag=f"att{b // HALF_BLOCKS}{b % HALF_BLOCKS}"
-            )
+            e_ps = banks.tile([P, ENTRIES], BF16, name=f"e_ps{b}", tag=att_bank)
             for mb in range(ENTRY_BLOCKS):
                 nc.tensor.transpose(
-                    p_ps[:, mb * P : (mb + 1) * P], pT_sb[:, mb * P : (mb + 1) * P], ident_bf16[:]
+                    e_ps[:, mb * P : (mb + 1) * P], eT_sb[:, mb * P : (mb + 1) * P], ident_bf16[:]
                 )
-            p_sb = held.tile([P, ENTRIES], BF16, name=f"p_sb{b}")
-            nc.scalar.copy(p_sb[:], p_ps[:])
-            out_ps = banks.tile([P, P], F32, name=f"out_ps{b}", tag=f"flip{b}")
+            e_sb = held.tile([P, ENTRIES], BF16, name=f"e_sb{b}")
+            nc.scalar.copy(e_sb[:], e_ps[:])
+            nc.vector.reciprocal(inverse[:, one], total[:, one])
+            inv_ps = banks.tile([P, P], F32, name=f"inv_ps{b}", tag=f"flip{b}")
+            nc.tensor.transpose(inv_ps[:], inverse[:, one].to_broadcast([P, P]), ident_f32[:])
+            inv_sb = held.tile([P, P], F32, name=f"inv_sb{b}")
+            nc.vector.tensor_copy(inv_sb[:], inv_ps[:])
+            num_ps = banks.tile([P, P], F32, name=f"num_ps{b}", tag=att_bank)
             for mb in range(ENTRY_BLOCKS):
                 nc.tensor.matmul(
-                    out_ps[:],
+                    num_ps[:],
                     kbT_sb[:, mb * P : (mb + 1) * P],
-                    p_sb[:, mb * P : (mb + 1) * P],
+                    e_sb[:, mb * P : (mb + 1) * P],
                     start=(mb == 0),
                     stop=(mb == ENTRY_BLOCKS - 1),
                 )
             out_sb = held.tile([P, P], F32, name=f"out_sb{b}")
-            nc.vector.tensor_copy(out_sb[:], out_ps[:])
+            nc.vector.tensor_tensor(out_sb[:], num_ps[:], inv_sb[:], MULT)
             nc.sync.dma_start(out[:, b * P : (b + 1) * P], out_sb[:])
 
         scores(0, 0)

@@ -27,12 +27,12 @@ def tile_encodertreespannn_kernel(tc, table, kb, offs, out):
         tc.tile_pool(name="held", bufs=1) as held,
         tc.psum_pool(name="banks", bufs=1) as banks,
     ):
+        table_sb = held.tile([P, WORDS], BF16, name="table_sb")
+        nc.sync.dma_start(table_sb[:], table)
         offsets = held.tile([P, LIST // 16], U16, name="offsets")
         nc.sync.dma_start(offsets[:], offs)
         kb_sb = held.tile([P, ENTRIES], BF16, name="kb_sb")
         nc.scalar.dma_start(kb_sb[:], kb)
-        table_sb = held.tile([P, WORDS], BF16, name="table_sb")
-        nc.sync.dma_start(table_sb[:], table)
 
         ident_f32 = held.tile([P, P], F32, name="ident_f32")
         make_identity(nc, ident_f32[:])

@@ -14,9 +14,7 @@ BAG = 4
 LIST = BAG * SPANS
 ENTRY_BLOCKS = ENTRIES // P
 SPAN_BLOCKS = SPANS // P
-HALVES = 2
-HALF = SPANS // HALVES
-HALF_BLOCKS = HALF // P
+PSUM_BANKS = 8
 
 FLOPS = 2 * P * ENTRIES * LIST + 2 * P * ENTRIES * SPANS
 
@@ -25,7 +23,9 @@ def tile_encodertreespannn_kernel(tc, table, kb, offs, out):
     nc = tc.nc
     with (
         tc.tile_pool(name="held", bufs=1) as held,
-        tc.psum_pool(name="banks", bufs=1) as banks,
+        tc.tile_pool(name="work", bufs=SPAN_BLOCKS) as work,
+        tc.psum_pool(name="ring_a", bufs=PSUM_BANKS // 2) as ring_a,
+        tc.psum_pool(name="ring_b", bufs=PSUM_BANKS // 2) as ring_b,
     ):
         table_sb = held.tile([P, WORDS], BF16, name="table_sb")
         nc.sync.dma_start(table_sb[:], table)
@@ -38,92 +38,89 @@ def tile_encodertreespannn_kernel(tc, table, kb, offs, out):
         make_identity(nc, ident_f32[:])
         ident_bf16 = held.tile([P, P], BF16, name="ident_bf16")
         make_identity(nc, ident_bf16[:])
-        warm = held.tile([P, 1], F32, name="warm")
-        nc.vector.memset(warm[:], 0.0)
+        warm_in = held.tile([P, 1], F32, name="warm_in")
+        nc.vector.memset(warm_in[:], 0.0)
         warm_out = held.tile([P, 1], F32, name="warm_out")
-        nc.scalar.activation(warm_out[:], warm[:], EXP)
+        nc.scalar.activation(warm_out[:], warm_in[:], EXP)
 
-
-        kbT_ps = banks.tile([P, ENTRIES], BF16, name="kbT_ps", tag="flip3")
+        kbT_ps = ring_b.tile([P, ENTRIES], BF16, name="kbT_ps", tag="bank")
         for mb in range(ENTRY_BLOCKS):
-            nc.tensor.transpose(
-                kbT_ps[:, mb * P : (mb + 1) * P], kb_sb[:, mb * P : (mb + 1) * P], ident_bf16[:]
-            )
+            entries = slice(mb * P, (mb + 1) * P)
+            nc.tensor.transpose(kbT_ps[:, entries], kb_sb[:, entries], ident_bf16[:])
         kbT_sb = held.tile([P, ENTRIES], BF16, name="kbT_sb")
         nc.vector.tensor_copy(kbT_sb[:], kbT_ps[:])
 
-        att_sb = {}
+        att_sb = [held.tile([P, SPANS], F32, name=f"att_sb{mb}") for mb in range(ENTRY_BLOCKS)]
         attT_ps = {}
         neg_max = held.tile([P, SPAN_BLOCKS], F32, name="neg_max")
         total = held.tile([P, SPAN_BLOCKS], F32, name="total")
         inverse = held.tile([P, SPAN_BLOCKS], F32, name="inverse")
 
-        def scores(h, mb):
-            att_ps = banks.tile([P, HALF], F32, name=f"att_ps{h}{mb}", tag=f"att{h}{mb}")
+        def scores(mb, first_block, blocks):
+            att_ps = ring_a.tile([P, blocks * P], F32, name="att_ps", tag="bank")
             for t in range(BAG):
-                first = (t * SPANS + h * HALF) // 16
+                first = (t * SPANS + first_block * P) // 16
                 nc.tensor.matmul(
                     att_ps[:],
                     kb_sb[:, mb * P : (mb + 1) * P],
-                    table_sb[:].indirect(offsets[:, first : first + HALF // 16]),
+                    table_sb[:].indirect(offsets[:, first : first + blocks * P // 16]),
                     start=(t == 0),
                     stop=(t == BAG - 1),
                 )
-            att_sb[h, mb] = held.tile([P, HALF], F32, name=f"att_sb{h}{mb}")
+            spans = slice(first_block * P, (first_block + blocks) * P)
             if mb == 0:
-                nc.scalar.copy(att_sb[h, mb][:], att_ps[:])
+                nc.scalar.copy(att_sb[mb][:, spans], att_ps[:])
             else:
-                nc.vector.tensor_copy(att_sb[h, mb][:], att_ps[:])
+                nc.vector.tensor_copy(att_sb[mb][:, spans], att_ps[:])
 
-        def flip(h):
-            for i in range(HALF_BLOCKS):
-                b = h * HALF_BLOCKS + i
-                attT_ps[b] = banks.tile([P, ENTRIES], F32, name=f"attT_ps{b}", tag=f"flip{b}")
-                for mb in range(ENTRY_BLOCKS):
-                    nc.tensor.transpose(
-                        attT_ps[b][:, mb * P : (mb + 1) * P],
-                        att_sb[h, mb][:, i * P : (i + 1) * P],
-                        ident_f32[:],
-                    )
+        def flip(b):
+            attT_ps[b] = ring_b.tile([P, ENTRIES], F32, name="attT_ps", tag="bank")
+            for mb in range(ENTRY_BLOCKS):
+                nc.tensor.transpose(
+                    attT_ps[b][:, mb * P : (mb + 1) * P],
+                    att_sb[mb][:, b * P : (b + 1) * P],
+                    ident_f32[:],
+                )
 
         def read_out(b):
             one = slice(b, b + 1)
-            att_bank = f"att{b // HALF_BLOCKS}{b % HALF_BLOCKS}"
             nc.vector.reduce_max(neg_max[:, one], attT_ps[b][:], X, negate=True)
-            eT_sb = held.tile([P, ENTRIES], BF16, name=f"eT_sb{b}")
+            eT_sb = work.tile([P, ENTRIES], BF16, name="eT_sb")
             nc.scalar.activation(
                 eT_sb[:], attT_ps[b][:], EXP, bias=neg_max[:, one], accum_out=total[:, one]
             )
-            e_ps = banks.tile([P, ENTRIES], BF16, name=f"e_ps{b}", tag=att_bank)
+            e_ps = ring_a.tile([P, ENTRIES], BF16, name="e_ps", tag="bank")
             for mb in range(ENTRY_BLOCKS):
-                nc.tensor.transpose(
-                    e_ps[:, mb * P : (mb + 1) * P], eT_sb[:, mb * P : (mb + 1) * P], ident_bf16[:]
-                )
-            e_sb = held.tile([P, ENTRIES], BF16, name=f"e_sb{b}")
+                entries = slice(mb * P, (mb + 1) * P)
+                nc.tensor.transpose(e_ps[:, entries], eT_sb[:, entries], ident_bf16[:])
+            e_sb = work.tile([P, ENTRIES], BF16, name="e_sb")
             nc.scalar.copy(e_sb[:], e_ps[:])
             nc.vector.reciprocal(inverse[:, one], total[:, one])
-            inv_ps = banks.tile([P, P], F32, name=f"inv_ps{b}", tag=f"flip{b}")
+            inv_ps = ring_b.tile([P, P], F32, name="inv_ps", tag="bank")
             nc.tensor.transpose(inv_ps[:], inverse[:, one].to_broadcast([P, P]), ident_f32[:])
-            inv_sb = held.tile([P, P], F32, name=f"inv_sb{b}")
+            inv_sb = work.tile([P, P], F32, name="inv_sb")
             nc.vector.tensor_copy(inv_sb[:], inv_ps[:])
-            num_ps = banks.tile([P, P], F32, name=f"num_ps{b}", tag=att_bank)
+            num_ps = ring_a.tile([P, P], F32, name="num_ps", tag="bank")
             for mb in range(ENTRY_BLOCKS):
+                entries = slice(mb * P, (mb + 1) * P)
                 nc.tensor.matmul(
                     num_ps[:],
-                    kbT_sb[:, mb * P : (mb + 1) * P],
-                    e_sb[:, mb * P : (mb + 1) * P],
+                    kbT_sb[:, entries],
+                    e_sb[:, entries],
                     start=(mb == 0),
                     stop=(mb == ENTRY_BLOCKS - 1),
                 )
-            out_sb = held.tile([P, P], F32, name=f"out_sb{b}")
+            out_sb = work.tile([P, P], F32, name="out_sb")
             nc.vector.tensor_tensor(out_sb[:], num_ps[:], inv_sb[:], MULT)
             nc.sync.dma_start(out[:, b * P : (b + 1) * P], out_sb[:])
 
-        scores(0, 0)
-        scores(0, 1)
-        scores(1, 0)
-        flip(0)
-        scores(1, 1)
-        flip(1)
+        half = SPAN_BLOCKS // 2
+        scores(0, 0, SPAN_BLOCKS)
+        scores(1, 0, half)
+        for b in range(half):
+            flip(b)
+        scores(1, half, half)
+        for b in range(half, SPAN_BLOCKS):
+            flip(b)
         for b in range(SPAN_BLOCKS):
             read_out(b)

@@ -14,7 +14,7 @@ BAG = 4
 LIST = BAG * SPANS
 ENTRY_BLOCKS = ENTRIES // P
 SPAN_BLOCKS = SPANS // P
-PSUM_BANKS = 8
+BACK_BANK = ("spare", "att00", "att10", "att12")
 
 FLOPS = 2 * P * ENTRIES * LIST + 2 * P * ENTRIES * SPANS
 
@@ -23,9 +23,7 @@ def tile_encodertreespannn_kernel(tc, table, kb, offs, out):
     nc = tc.nc
     with (
         tc.tile_pool(name="held", bufs=1) as held,
-        tc.tile_pool(name="work", bufs=SPAN_BLOCKS) as work,
-        tc.psum_pool(name="ring_a", bufs=PSUM_BANKS // 2) as ring_a,
-        tc.psum_pool(name="ring_b", bufs=PSUM_BANKS // 2) as ring_b,
+        tc.psum_pool(name="banks", bufs=1) as banks,
     ):
         table_sb = held.tile([P, WORDS], BF16, name="table_sb")
         nc.sync.dma_start(table_sb[:], table)
@@ -43,7 +41,7 @@ def tile_encodertreespannn_kernel(tc, table, kb, offs, out):
         warm_out = held.tile([P, 1], F32, name="warm_out")
         nc.scalar.activation(warm_out[:], warm_in[:], EXP)
 
-        kbT_ps = ring_b.tile([P, ENTRIES], BF16, name="kbT_ps", tag="bank")
+        kbT_ps = banks.tile([P, ENTRIES], BF16, name="kbT_ps", tag="flip3")
         for mb in range(ENTRY_BLOCKS):
             entries = slice(mb * P, (mb + 1) * P)
             nc.tensor.transpose(kbT_ps[:, entries], kb_sb[:, entries], ident_bf16[:])
@@ -57,7 +55,9 @@ def tile_encodertreespannn_kernel(tc, table, kb, offs, out):
         inverse = held.tile([P, SPAN_BLOCKS], F32, name="inverse")
 
         def scores(mb, first_block, blocks):
-            att_ps = ring_a.tile([P, blocks * P], F32, name="att_ps", tag="bank")
+            att_ps = banks.tile(
+                [P, blocks * P], F32, name=f"att_ps{mb}{first_block}", tag=f"att{mb}{first_block}"
+            )
             for t in range(BAG):
                 first = (t * SPANS + first_block * P) // 16
                 nc.tensor.matmul(
@@ -74,7 +74,7 @@ def tile_encodertreespannn_kernel(tc, table, kb, offs, out):
                 nc.vector.tensor_copy(att_sb[mb][:, spans], att_ps[:])
 
         def flip(b):
-            attT_ps[b] = ring_b.tile([P, ENTRIES], F32, name="attT_ps", tag="bank")
+            attT_ps[b] = banks.tile([P, ENTRIES], F32, name=f"attT_ps{b}", tag=f"flip{b}")
             for mb in range(ENTRY_BLOCKS):
                 nc.tensor.transpose(
                     attT_ps[b][:, mb * P : (mb + 1) * P],
@@ -85,22 +85,22 @@ def tile_encodertreespannn_kernel(tc, table, kb, offs, out):
         def read_out(b):
             one = slice(b, b + 1)
             nc.vector.reduce_max(neg_max[:, one], attT_ps[b][:], X, negate=True)
-            eT_sb = work.tile([P, ENTRIES], BF16, name="eT_sb")
+            eT_sb = held.tile([P, ENTRIES], BF16, name=f"eT_sb{b}")
             nc.scalar.activation(
                 eT_sb[:], attT_ps[b][:], EXP, bias=neg_max[:, one], accum_out=total[:, one]
             )
-            e_ps = ring_a.tile([P, ENTRIES], BF16, name="e_ps", tag="bank")
+            e_ps = banks.tile([P, ENTRIES], BF16, name=f"e_ps{b}", tag=BACK_BANK[b])
             for mb in range(ENTRY_BLOCKS):
                 entries = slice(mb * P, (mb + 1) * P)
                 nc.tensor.transpose(e_ps[:, entries], eT_sb[:, entries], ident_bf16[:])
-            e_sb = work.tile([P, ENTRIES], BF16, name="e_sb")
+            e_sb = held.tile([P, ENTRIES], BF16, name=f"e_sb{b}")
             nc.scalar.copy(e_sb[:], e_ps[:])
             nc.vector.reciprocal(inverse[:, one], total[:, one])
-            inv_ps = ring_b.tile([P, P], F32, name="inv_ps", tag="bank")
+            inv_ps = banks.tile([P, P], F32, name=f"inv_ps{b}", tag=f"flip{b}")
             nc.tensor.transpose(inv_ps[:], inverse[:, one].to_broadcast([P, P]), ident_f32[:])
-            inv_sb = work.tile([P, P], F32, name="inv_sb")
+            inv_sb = held.tile([P, P], F32, name=f"inv_sb{b}")
             nc.vector.tensor_copy(inv_sb[:], inv_ps[:])
-            num_ps = ring_a.tile([P, P], F32, name="num_ps", tag="bank")
+            num_ps = banks.tile([P, P], F32, name=f"num_ps{b}", tag=BACK_BANK[b])
             for mb in range(ENTRY_BLOCKS):
                 entries = slice(mb * P, (mb + 1) * P)
                 nc.tensor.matmul(
@@ -110,7 +110,7 @@ def tile_encodertreespannn_kernel(tc, table, kb, offs, out):
                     start=(mb == 0),
                     stop=(mb == ENTRY_BLOCKS - 1),
                 )
-            out_sb = work.tile([P, P], F32, name="out_sb")
+            out_sb = held.tile([P, P], F32, name=f"out_sb{b}")
             nc.vector.tensor_tensor(out_sb[:], num_ps[:], inv_sb[:], MULT)
             nc.sync.dma_start(out[:, b * P : (b + 1) * P], out_sb[:])
 

@@ -4,7 +4,6 @@ from concourse.masks import make_identity
 BF16, F32, U16 = mybir.dt.bfloat16, mybir.dt.float32, mybir.dt.uint16
 EXP = mybir.ActivationFunctionType.Exp
 MULT = mybir.AluOpType.mult
-X = mybir.AxisListType.X
 
 P = 128
 WORDS = 1024
@@ -13,8 +12,8 @@ SPANS = 512
 BAG = 4
 LIST = BAG * SPANS
 ENTRY_BLOCKS = ENTRIES // P
-SPAN_BLOCKS = SPANS // P
-BACK_BANK = ("spare", "att00", "att10", "att12")
+EARLY = (0, 3)
+LATE = (3, 1)
 
 FLOPS = 2 * P * ENTRIES * LIST + 2 * P * ENTRIES * SPANS
 
@@ -32,32 +31,29 @@ def tile_encodertreespannn_kernel(tc, table, kb, offs, out):
         kb_sb = held.tile([P, ENTRIES], BF16, name="kb_sb")
         nc.scalar.dma_start(kb_sb[:], kb)
 
-        ident_f32 = held.tile([P, P], F32, name="ident_f32")
-        make_identity(nc, ident_f32[:])
         ident_bf16 = held.tile([P, P], BF16, name="ident_bf16")
         make_identity(nc, ident_bf16[:])
+        ident_f32 = held.tile([P, P], F32, name="ident_f32")
+        make_identity(nc, ident_f32[:])
+        ones = held.tile([P, 1], BF16, name="ones")
+        nc.vector.memset(ones[:], 1.0)
         warm_in = held.tile([P, 1], F32, name="warm_in")
         nc.vector.memset(warm_in[:], 0.0)
         warm_out = held.tile([P, 1], F32, name="warm_out")
         nc.scalar.activation(warm_out[:], warm_in[:], EXP)
 
-        kbT_ps = banks.tile([P, ENTRIES], BF16, name="kbT_ps", tag="flip3")
+        kbT_ps = banks.tile([P, ENTRIES], BF16, name="kbT_ps", tag="bank0")
         for mb in range(ENTRY_BLOCKS):
             entries = slice(mb * P, (mb + 1) * P)
             nc.tensor.transpose(kbT_ps[:, entries], kb_sb[:, entries], ident_bf16[:])
         kbT_sb = held.tile([P, ENTRIES], BF16, name="kbT_sb")
         nc.vector.tensor_copy(kbT_sb[:], kbT_ps[:])
 
-        att_sb = [held.tile([P, SPANS], F32, name=f"att_sb{mb}") for mb in range(ENTRY_BLOCKS)]
-        attT_ps = {}
-        neg_max = held.tile([P, SPAN_BLOCKS], F32, name="neg_max")
-        total = held.tile([P, SPAN_BLOCKS], F32, name="total")
-        inverse = held.tile([P, SPAN_BLOCKS], F32, name="inverse")
+        e_sb = [held.tile([P, SPANS], BF16, name=f"e_sb{mb}") for mb in range(ENTRY_BLOCKS)]
 
-        def scores(mb, first_block, blocks):
-            att_ps = banks.tile(
-                [P, blocks * P], F32, name=f"att_ps{mb}{first_block}", tag=f"att{mb}{first_block}"
-            )
+        def scores(mb, part, tag):
+            first_block, blocks = part
+            att_ps = banks.tile([P, blocks * P], F32, name=f"att_ps_{tag}", tag=tag)
             for t in range(BAG):
                 first = (t * SPANS + first_block * P) // 16
                 nc.tensor.matmul(
@@ -68,59 +64,54 @@ def tile_encodertreespannn_kernel(tc, table, kb, offs, out):
                     stop=(t == BAG - 1),
                 )
             spans = slice(first_block * P, (first_block + blocks) * P)
-            if mb == 0:
-                nc.scalar.copy(att_sb[mb][:, spans], att_ps[:])
-            else:
-                nc.vector.tensor_copy(att_sb[mb][:, spans], att_ps[:])
+            nc.scalar.activation(e_sb[mb][:, spans], att_ps[:], EXP)
 
-        def flip(b):
-            attT_ps[b] = banks.tile([P, ENTRIES], F32, name=f"attT_ps{b}", tag=f"flip{b}")
+        def sums_and_products(part, sum_tag, num_tag):
+            first_block, blocks = part
+            sum_ps = banks.tile([P, blocks], F32, name=f"sum_ps_{sum_tag}", tag=sum_tag)
+            for b in range(blocks):
+                spans = slice((first_block + b) * P, (first_block + b + 1) * P)
+                for mb in range(ENTRY_BLOCKS):
+                    nc.tensor.matmul(
+                        sum_ps[:, b : b + 1],
+                        e_sb[mb][:, spans],
+                        ones[:],
+                        start=(mb == 0),
+                        stop=(mb == ENTRY_BLOCKS - 1),
+                    )
+            inverse = held.tile([P, blocks], F32, name=f"inverse_{sum_tag}")
+            nc.vector.reciprocal(inverse[:], sum_ps[:])
+            spans = slice(first_block * P, (first_block + blocks) * P)
+            num_ps = banks.tile([P, blocks * P], F32, name=f"num_ps_{num_tag}", tag=num_tag)
             for mb in range(ENTRY_BLOCKS):
-                nc.tensor.transpose(
-                    attT_ps[b][:, mb * P : (mb + 1) * P],
-                    att_sb[mb][:, b * P : (b + 1) * P],
-                    ident_f32[:],
-                )
-
-        def read_out(b):
-            one = slice(b, b + 1)
-            nc.vector.reduce_max(neg_max[:, one], attT_ps[b][:], X, negate=True)
-            eT_sb = held.tile([P, ENTRIES], BF16, name=f"eT_sb{b}")
-            nc.scalar.activation(
-                eT_sb[:], attT_ps[b][:], EXP, bias=neg_max[:, one], accum_out=total[:, one]
-            )
-            e_ps = banks.tile([P, ENTRIES], BF16, name=f"e_ps{b}", tag=BACK_BANK[b])
-            for mb in range(ENTRY_BLOCKS):
-                entries = slice(mb * P, (mb + 1) * P)
-                nc.tensor.transpose(e_ps[:, entries], eT_sb[:, entries], ident_bf16[:])
-            e_sb = held.tile([P, ENTRIES], BF16, name=f"e_sb{b}")
-            nc.scalar.copy(e_sb[:], e_ps[:])
-            nc.vector.reciprocal(inverse[:, one], total[:, one])
-            inv_ps = banks.tile([P, P], F32, name=f"inv_ps{b}", tag=f"flip{b}")
-            nc.tensor.transpose(inv_ps[:], inverse[:, one].to_broadcast([P, P]), ident_f32[:])
-            inv_sb = held.tile([P, P], F32, name=f"inv_sb{b}")
-            nc.vector.tensor_copy(inv_sb[:], inv_ps[:])
-            num_ps = banks.tile([P, P], F32, name=f"num_ps{b}", tag=BACK_BANK[b])
-            for mb in range(ENTRY_BLOCKS):
-                entries = slice(mb * P, (mb + 1) * P)
                 nc.tensor.matmul(
                     num_ps[:],
-                    kbT_sb[:, entries],
-                    e_sb[:, entries],
+                    kbT_sb[:, mb * P : (mb + 1) * P],
+                    e_sb[mb][:, spans],
                     start=(mb == 0),
                     stop=(mb == ENTRY_BLOCKS - 1),
                 )
-            out_sb = held.tile([P, P], F32, name=f"out_sb{b}")
-            nc.vector.tensor_tensor(out_sb[:], num_ps[:], inv_sb[:], MULT)
-            nc.sync.dma_start(out[:, b * P : (b + 1) * P], out_sb[:])
+            num_sb = held.tile([P, blocks * P], F32, name=f"num_sb_{num_tag}")
+            nc.scalar.copy(num_sb[:], num_ps[:])
+            return inverse, num_sb
 
-        half = SPAN_BLOCKS // 2
-        scores(0, 0, SPAN_BLOCKS)
-        scores(1, 0, half)
-        for b in range(half):
-            flip(b)
-        scores(1, half, half)
-        for b in range(half, SPAN_BLOCKS):
-            flip(b)
-        for b in range(SPAN_BLOCKS):
-            read_out(b)
+        def scale_and_store(part, inverse, num_sb, tag):
+            first_block, blocks = part
+            inv_ps = banks.tile([P, blocks * P], F32, name=f"inv_ps_{tag}", tag=tag)
+            for b in range(blocks):
+                nc.tensor.transpose(
+                    inv_ps[:, b * P : (b + 1) * P],
+                    inverse[:, b : b + 1].to_broadcast([P, P]),
+                    ident_f32[:],
+                )
+            out_sb = held.tile([P, blocks * P], F32, name=f"out_sb_{tag}")
+            nc.vector.tensor_tensor(out_sb[:], inv_ps[:], num_sb[:], MULT)
+            nc.sync.dma_start(out[:, first_block * P : (first_block + blocks) * P], out_sb[:])
+
+        scores(0, (0, SPANS // P), "bank1")
+        scores(1, EARLY, "bank2")
+        scores(1, LATE, "bank3")
+        early = sums_and_products(EARLY, "bank0", "bank1")
+        late = sums_and_products(LATE, "bank4", "bank5")
+        scale_and_store(EARLY, early[0], early[1], "bank2")
+        scale_and_store(LATE, late[0], late[1], "bank6")

@@ -3,7 +3,7 @@ from concourse.masks import make_identity
 
 BF16, F32, U16 = mybir.dt.bfloat16, mybir.dt.float32, mybir.dt.uint16
 EXP = mybir.ActivationFunctionType.Exp
-MULT = mybir.AluOpType.mult
+MULT, ADD, IS_EQUAL = mybir.AluOpType.mult, mybir.AluOpType.add, mybir.AluOpType.is_equal
 
 P = 128
 WORDS = 1024
@@ -12,6 +12,7 @@ SPANS = 512
 BAG = 4
 LIST = BAG * SPANS
 ENTRY_BLOCKS = ENTRIES // P
+SQUARE = 32
 EARLY = (0, 3)
 LATE = (3, 1)
 
@@ -31,8 +32,18 @@ def tile_encodertreespannn_kernel(tc, table, kb, offs, out):
         kb_sb = held.tile([P, ENTRIES], BF16, name="kb_sb")
         nc.scalar.dma_start(kb_sb[:], kb)
 
+        all_ones = held.tile([P, P], F32, name="all_ones")
+        nc.vector.memset(all_ones[:], 1.0)
+        column = held.tile([P, P], F32, name="column", align_bytes=64)
+        nc.vector.tensor_tensor_scan(column[:], all_ones[:], all_ones[:], -1.0, MULT, ADD)
+        flipped = held.tile([P, P], F32, name="flipped", align_bytes=64)
+        nc.vector.transpose(flipped[:], column[:])
         ident_bf16 = held.tile([P, P], BF16, name="ident_bf16")
-        make_identity(nc, ident_bf16[:])
+        for g in range(P // SQUARE):
+            rows = slice(g * SQUARE, (g + 1) * SQUARE)
+            nc.vector.tensor_scalar(
+                ident_bf16[rows, :], column[rows, :], flipped[rows, g * SQUARE : g * SQUARE + 1], None, IS_EQUAL
+            )
         ident_f32 = held.tile([P, P], F32, name="ident_f32")
         make_identity(nc, ident_f32[:])
         ones = held.tile([P, 1], BF16, name="ones")

@@ -1,5 +1,4 @@
 import concourse.mybir as mybir
-from concourse.masks import make_identity
 
 BF16, F32, U16 = mybir.dt.bfloat16, mybir.dt.float32, mybir.dt.uint16
 EXP = mybir.ActivationFunctionType.Exp
@@ -45,7 +44,7 @@ def tile_encodertreespannn_kernel(tc, table, kb, offs, out):
                 ident_bf16[rows, :], column[rows, :], flipped[rows, g * SQUARE : g * SQUARE + 1], None, IS_EQUAL
             )
         ident_f32 = held.tile([P, P], F32, name="ident_f32")
-        make_identity(nc, ident_f32[:])
+        nc.vector.tensor_copy(ident_f32[:], ident_bf16[:])
         ones = held.tile([P, 1], BF16, name="ones")
         nc.vector.memset(ones[:], 1.0)
         warm_in = held.tile([P, 1], F32, name="warm_in")

@@ -47,10 +47,6 @@ def tile_encodertreespannn_kernel(tc, table, kb, offs, out):
         nc.vector.tensor_copy(ident_f32[:], ident_bf16[:])
         ones = held.tile([P, 1], BF16, name="ones")
         nc.vector.memset(ones[:], 1.0)
-        warm_in = held.tile([P, 1], F32, name="warm_in")
-        nc.vector.memset(warm_in[:], 0.0)
-        warm_out = held.tile([P, 1], F32, name="warm_out")
-        nc.scalar.activation(warm_out[:], warm_in[:], EXP)
 
         kbT_ps = banks.tile([P, ENTRIES], BF16, name="kbT_ps", tag="bank0")
         for mb in range(ENTRY_BLOCKS):

@@ -12,8 +12,8 @@ BAG = 4
 LIST = BAG * SPANS
 ENTRY_BLOCKS = ENTRIES // P
 SQUARE = 32
-EARLY = (0, 3)
-LATE = (3, 1)
+EARLY = (0, 2)
+LATE = (2, 2)
 
 FLOPS = 2 * P * ENTRIES * LIST + 2 * P * ENTRIES * SPANS
 

@@ -29,7 +29,7 @@ def tile_encodertreespannn_kernel(tc, table, kb, offs, out):
         offsets = held.tile([P, LIST // 16], U16, name="offsets")
         nc.sync.dma_start(offsets[:], offs)
         kb_sb = held.tile([P, ENTRIES], BF16, name="kb_sb")
-        nc.scalar.dma_start(kb_sb[:], kb)
+        nc.sync.dma_start(kb_sb[:], kb)
 
         all_ones = held.tile([P, P], F32, name="all_ones")
         nc.vector.memset(all_ones[:], 1.0)
@@ -48,12 +48,14 @@ def tile_encodertreespannn_kernel(tc, table, kb, offs, out):
         ones = held.tile([P, 1], BF16, name="ones")
         nc.vector.memset(ones[:], 1.0)
 
-        kbT_ps = banks.tile([P, ENTRIES], BF16, name="kbT_ps", tag="bank0")
-        for mb in range(ENTRY_BLOCKS):
-            entries = slice(mb * P, (mb + 1) * P)
-            nc.tensor.transpose(kbT_ps[:, entries], kb_sb[:, entries], ident_bf16[:])
         kbT_sb = held.tile([P, ENTRIES], BF16, name="kbT_sb")
-        nc.vector.tensor_copy(kbT_sb[:], kbT_ps[:])
+
+        def flip_kb():
+            kbT_ps = banks.tile([P, ENTRIES], BF16, name="kbT_ps", tag="bank0")
+            for mb in range(ENTRY_BLOCKS):
+                entries = slice(mb * P, (mb + 1) * P)
+                nc.tensor.transpose(kbT_ps[:, entries], kb_sb[:, entries], ident_bf16[:])
+            nc.vector.tensor_copy(kbT_sb[:], kbT_ps[:])
 
         e_sb = [held.tile([P, SPANS], BF16, name=f"e_sb{mb}") for mb in range(ENTRY_BLOCKS)]
 
@@ -115,6 +117,7 @@ def tile_encodertreespannn_kernel(tc, table, kb, offs, out):
             nc.sync.dma_start(out[:, first_block * P : (first_block + blocks) * P], out_sb[:])
 
         scores(0, (0, SPANS // P), "bank1")
+        flip_kb()
         scores(1, EARLY, "bank2")
         scores(1, LATE, "bank3")
         early = sums_and_products(EARLY, "bank0", "bank1")

@@ -25,11 +25,12 @@ def tile_encodertreespannn_kernel(tc, table, kb, offs, out):
         tc.psum_pool(name="banks", bufs=1) as banks,
     ):
         table_sb = held.tile([P, WORDS], BF16, name="table_sb")
-        nc.sync.dma_start(table_sb[:], table)
+        nc.sync.dma_start(table_sb[:, : WORDS // 2], table[:, : WORDS // 2])
+        nc.scalar.dma_start(table_sb[:, WORDS // 2 :], table[:, WORDS // 2 :])
         offsets = held.tile([P, LIST // 16], U16, name="offsets")
         nc.sync.dma_start(offsets[:], offs)
         kb_sb = held.tile([P, ENTRIES], BF16, name="kb_sb")
-        nc.sync.dma_start(kb_sb[:], kb)
+        nc.scalar.dma_start(kb_sb[:], kb)
 
         all_ones = held.tile([P, P], F32, name="all_ones")
         nc.vector.memset(all_ones[:], 1.0)

import concourse.mybir as mybir

BF16, F32, U16 = mybir.dt.bfloat16, mybir.dt.float32, mybir.dt.uint16
EXP = mybir.ActivationFunctionType.Exp
MULT, ADD, IS_EQUAL = mybir.AluOpType.mult, mybir.AluOpType.add, mybir.AluOpType.is_equal

P = 128
WORDS = 1024
ENTRIES = 256
SPANS = 512
BAG = 4
LIST = BAG * SPANS
ENTRY_BLOCKS = ENTRIES // P
SQUARE = 32
EARLY = (0, 2)
LATE = (2, 2)

FLOPS = 2 * P * ENTRIES * LIST + 2 * P * ENTRIES * SPANS


def tile_encodertreespannn_kernel(tc, table, kb, offs, out):
    nc = tc.nc
    with (
        tc.tile_pool(name="held", bufs=1) as held,
        tc.psum_pool(name="banks", bufs=1) as banks,
    ):
        table_sb = held.tile([P, WORDS], BF16, name="table_sb")
        nc.sync.dma_start(table_sb[:, : WORDS // 2], table[:, : WORDS // 2])
        nc.scalar.dma_start(table_sb[:, WORDS // 2 :], table[:, WORDS // 2 :])
        offsets = held.tile([P, LIST // 16], U16, name="offsets")
        nc.sync.dma_start(offsets[:], offs)
        kb_sb = held.tile([P, ENTRIES], BF16, name="kb_sb")
        nc.scalar.dma_start(kb_sb[:], kb)

        all_ones = held.tile([P, P], F32, name="all_ones")
        nc.vector.memset(all_ones[:], 1.0)
        column = held.tile([P, P], F32, name="column", align_bytes=64)
        nc.vector.tensor_tensor_scan(column[:], all_ones[:], all_ones[:], -1.0, MULT, ADD)
        flipped = held.tile([P, P], F32, name="flipped", align_bytes=64)
        nc.vector.transpose(flipped[:], column[:])
        ident_bf16 = held.tile([P, P], BF16, name="ident_bf16")
        for g in range(P // SQUARE):
            rows = slice(g * SQUARE, (g + 1) * SQUARE)
            nc.vector.tensor_scalar(
                ident_bf16[rows, :], column[rows, :], flipped[rows, g * SQUARE : g * SQUARE + 1], None, IS_EQUAL
            )
        ident_f32 = held.tile([P, P], F32, name="ident_f32")
        nc.vector.tensor_copy(ident_f32[:], ident_bf16[:])
        ones = held.tile([P, 1], BF16, name="ones")
        nc.vector.memset(ones[:], 1.0)

        kbT_sb = held.tile([P, ENTRIES], BF16, name="kbT_sb")

        def flip_kb():
            kbT_ps = banks.tile([P, ENTRIES], BF16, name="kbT_ps", tag="bank0")
            for mb in range(ENTRY_BLOCKS):
                entries = slice(mb * P, (mb + 1) * P)
                nc.tensor.transpose(kbT_ps[:, entries], kb_sb[:, entries], ident_bf16[:])
            nc.vector.tensor_copy(kbT_sb[:], kbT_ps[:])

        e_sb = [held.tile([P, SPANS], BF16, name=f"e_sb{mb}") for mb in range(ENTRY_BLOCKS)]

        def scores(mb, part, tag):
            first_block, blocks = part
            att_ps = banks.tile([P, blocks * P], F32, name=f"att_ps_{tag}", tag=tag)
            for t in range(BAG):
                first = (t * SPANS + first_block * P) // 16
                nc.tensor.matmul(
                    att_ps[:],
                    kb_sb[:, mb * P : (mb + 1) * P],
                    table_sb[:].indirect(offsets[:, first : first + blocks * P // 16]),
                    start=(t == 0),
                    stop=(t == BAG - 1),
                )
            spans = slice(first_block * P, (first_block + blocks) * P)
            nc.scalar.activation(e_sb[mb][:, spans], att_ps[:], EXP)

        def sums_and_products(part, sum_tag, num_tag):
            first_block, blocks = part
            sum_ps = banks.tile([P, blocks], F32, name=f"sum_ps_{sum_tag}", tag=sum_tag)
            for b in range(blocks):
                spans = slice((first_block + b) * P, (first_block + b + 1) * P)
                for mb in range(ENTRY_BLOCKS):
                    nc.tensor.matmul(
                        sum_ps[:, b : b + 1],
                        e_sb[mb][:, spans],
                        ones[:],
                        start=(mb == 0),
                        stop=(mb == ENTRY_BLOCKS - 1),
                    )
            inverse = held.tile([P, blocks], F32, name=f"inverse_{sum_tag}")
            nc.vector.reciprocal(inverse[:], sum_ps[:])
            spans = slice(first_block * P, (first_block + blocks) * P)
            num_ps = banks.tile([P, blocks * P], F32, name=f"num_ps_{num_tag}", tag=num_tag)
            for mb in range(ENTRY_BLOCKS):
                nc.tensor.matmul(
                    num_ps[:],
                    kbT_sb[:, mb * P : (mb + 1) * P],
                    e_sb[mb][:, spans],
                    start=(mb == 0),
                    stop=(mb == ENTRY_BLOCKS - 1),
                )
            num_sb = held.tile([P, blocks * P], F32, name=f"num_sb_{num_tag}")
            nc.scalar.copy(num_sb[:], num_ps[:])
            return inverse, num_sb

        def scale_and_store(part, inverse, num_sb, tag):
            first_block, blocks = part
            inv_ps = banks.tile([P, blocks * P], F32, name=f"inv_ps_{tag}", tag=tag)
            for b in range(blocks):
                nc.tensor.transpose(
                    inv_ps[:, b * P : (b + 1) * P],
                    inverse[:, b : b + 1].to_broadcast([P, P]),
                    ident_f32[:],
                )
            out_sb = held.tile([P, blocks * P], F32, name=f"out_sb_{tag}")
            nc.vector.tensor_tensor(out_sb[:], inv_ps[:], num_sb[:], MULT)
            nc.sync.dma_start(out[:, first_block * P : (first_block + blocks) * P], out_sb[:])

        scores(0, (0, SPANS // P), "bank1")
        flip_kb()
        scores(1, EARLY, "bank2")
        scores(1, LATE, "bank3")
        early = sums_and_products(EARLY, "bank0", "bank1")
        late = sums_and_products(LATE, "bank4", "bank5")
        scale_and_store(EARLY, early[0], early[1], "bank2")
        scale_and_store(LATE, late[0], late[1], "bank6")
